import numpy as np
import ml_dtypes


def mxq(x, axis, fmt="e4m3"):
    dtype, down = {"e4m3": (ml_dtypes.float8_e4m3fn, 7), "e5m2": (ml_dtypes.float8_e5m2, 14)}[fmt]
    v = np.moveaxis(np.asarray(x, np.float32).astype(ml_dtypes.bfloat16).astype(np.float64), axis, -1)
    blocks = v.reshape(v.shape[:-1] + (-1, 32))
    amax = np.abs(blocks).max(-1, keepdims=True)
    byte = np.maximum(np.where(amax > 0, np.frexp(amax)[1] - 1 + 127, 0) - down, 1)
    scale = np.exp2(byte - 127.0)
    codes = (blocks / scale).astype(np.float32).astype(dtype).astype(np.float64)
    return np.moveaxis((codes * scale).reshape(v.shape), -1, axis)


WIDE = False


def mx_kscale(k):
    if not WIDE:
        return np.ones(k)
    levels = np.array([20, -20, 10, -10, 0])
    a = np.random.permutation(np.resize(levels, k // 512 * 4)).reshape(k // 512, 4)
    idx = np.arange(k)
    return np.exp2(a[idx // 512, idx % 128 // 32])


BF16 = ml_dtypes.bfloat16


def bf(x):
    return np.asarray(x, np.float32).astype(BF16)


def f64(x):
    return np.asarray(x).astype(np.float64)


N, FA, FB, O = 4096, 512, 512, 512

GRID = 65536.0


def _grid(v):
    return np.round(v * GRID) / GRID


def setup_inputs():
    u = mx_kscale(O)
    xa = _grid(np.random.standard_normal((N, FA)))
    xb = _grid(np.random.standard_normal((N, FB)))
    y = np.random.uniform(0.0, 1.0, (N, O))
    wa = _grid(np.random.standard_normal((FA, O)) * 0.9 / np.sqrt(FA)) / u
    wb = _grid(np.random.standard_normal((FB, O)) * 0.9 / np.sqrt(FB))
    g = np.random.standard_normal((N, O)) * np.exp2(np.random.randint(-12, 1, (N, 1))) * 32.0 * u
    return {"xa": bf(xa), "xb": bf(xb), "y": bf(y), "wa": bf(wa), "wb": bf(wb), "grad_out": bf(g)}


def reference(xa, xb, y, wa, wb, grad_out):
    p = mxq(f64(grad_out), 1, "e5m2") @ mxq(f64(wa), 1, "e4m3").T
    return 0.25 * p

@@ -1,0 +1,169 @@
+from contextlib import ExitStack
+
+import concourse.mybir as mybir
+from concourse.masks import make_identity
+
+F32 = mybir.dt.float32
+BF16 = mybir.dt.bfloat16
+U32 = mybir.dt.uint32
+U8 = mybir.dt.uint8
+E4M3X4 = mybir.dt.float8_e4m3fn_x4
+E5M2X4 = mybir.dt.float8_e5m2_x4
+COPY = mybir.ActivationFunctionType.Copy
+
+P = 128
+N_TOK = 4096
+K = 512
+FA = 512
+TILES = N_TOK // P
+GROUP = 4
+GROUPS = TILES // GROUP
+WORDS = K // 2
+
+FLOPS = 2 * N_TOK * K * FA
+BYTES = N_TOK * K * 2 + FA * K * 2 + N_TOK * FA * 4
+
+PINNED = True
+LOADS = [(0, 4), (4, 8), (8, 12), (12, 16), (16, 24), (24, 32)]
+
+
+def tile_ssheaggregatorlayer_t_kernel(tc, xa, xb, y, wa, wb, grad_out, out):
+    nc = tc.nc
+    with ExitStack() as ctx:
+        keep = ctx.enter_context(tc.tile_pool(name="keep", bufs=1))
+        xt_pool = ctx.enter_context(tc.psum_pool(name="xtp", bufs=4))
+        acc_pool = ctx.enter_context(tc.psum_pool(name="accp", bufs=4))
+        if PINNED:
+            ctx.enter_context(tc.manual_schedule())
+
+        g_view = grad_out.rearrange("(p t) o -> p t o", t=TILES)
+        out_view = out.rearrange("(p t) f -> p t f", t=TILES)
+
+        w_sb = keep.tile([P, GROUP * K], BF16, name="w_sb")
+        nc.sync.dma_start(
+            out=w_sb[:].rearrange("p (j o) -> p j o", o=K),
+            in_=wa.rearrange("(j p) o -> p j o", p=P),
+        )
+        src_of_tile = {}
+        for c, (t0, t1) in enumerate(LOADS):
+            g_sb = keep.tile([P, (t1 - t0) * K], BF16, name="g_sb%d" % c)
+            nc.sync.dma_start(
+                out=g_sb[:].rearrange("p (t o) -> p t o", o=K),
+                in_=g_view[:, t0:t1, :],
+            )
+            for t in range(t0, t1):
+                src_of_tile[t] = (g_sb[:].bitcast(F32), t - t0)
+
+        ident = keep.tile([P, P], F32, name="ident")
+        make_identity(nc, ident[:])
+        warm = keep.tile([P, 8], F32, name="warm")
+        nc.vector.memset(warm[:], 0.0)
+        nc.scalar.activation(out=warm[:], in_=warm[:], func=COPY, scale=0.25)
+
+        w_words = w_sb[:].bitcast(F32)
+        banks = {}
+        grouped = {}
+        codes = {}
+        scales = {}
+        accs = {}
+        o_sb = {}
+
+        def source(n, s):
+            if n == "w":
+                return w_words, s
+            return src_of_tile[GROUP * n + s]
+
+        def tr(n):
+            grouped[n] = keep.tile([P, GROUP * K], BF16, name="grouped_%s" % n, align_bytes=64)
+            for h in range(2):
+                xt = xt_pool.tile([P, 2, 2, P], F32, name="xt")
+                banks[(n, h)] = xt
+                for s in range(2):
+                    words, local = source(n, 2 * h + s)
+                    for u in range(2):
+                        col = local * WORDS + u * P
+                        nc.tensor.transpose(xt[:, s, u, :], words[:, col : col + P], ident[:])
+
+        def cp(n, h, on_vector):
+            dst = grouped[n][:].bitcast(F32)[:, h * K : (h + 1) * K]
+            dst = dst.rearrange("p (s n u) -> p s n u", s=2, u=2)
+            src = banks[(n, h)][:].rearrange("p s u n -> p s n u")
+            if on_vector:
+                nc.vector.tensor_copy(out=dst, in_=src)
+            else:
+                nc.scalar.copy(out=dst, in_=src)
+
+        def qz(n):
+            codes[n] = keep.tile([P, GROUP * P], U32, name="codes_%s" % n, align_bytes=64)
+            scales[n] = keep.tile([P, GROUP * P], U8, name="scales_%s" % n, align_bytes=64)
+            fmt = E4M3X4 if n == "w" else E5M2X4
+            nc.vector.quantize_mx(out=codes[n][:].bitcast(fmt), scales=scales[n][:], in_=grouped[n][:])
+
+        def mx(n):
+            for s in range(GROUP):
+                acc = acc_pool.tile([P, FA], F32, name="acc")
+                accs[(n, s)] = acc
+                cols = slice(s * P, (s + 1) * P)
+                nc.tensor.matmul_mx(
+                    out=acc[:],
+                    lhsT=codes[n][:, cols].bitcast(E5M2X4),
+                    lhsT_scale=scales[n][:, cols],
+                    rhs=codes["w"][:].bitcast(E4M3X4),
+                    rhs_scale=scales["w"][:],
+                    start=True,
+                    stop=True,
+                )
+
+        def ev(n, s, on_vector):
+            if s == 0:
+                o_sb[n] = keep.tile([P, GROUP * FA], F32, name="o_sb%d" % n)
+            dst = o_sb[n][:, s * FA : (s + 1) * FA]
+            if on_vector:
+                nc.vector.tensor_scalar_mul(out=dst, in0=accs[(n, s)][:], scalar1=0.25)
+            else:
+                nc.scalar.activation(out=dst, in_=accs[(n, s)][:], func=COPY, scale=0.25)
+
+        def st(n):
+            nc.sync.dma_start(
+                out=out_view[:, GROUP * n : GROUP * (n + 1), :],
+                in_=o_sb[n][:].rearrange("p (t f) -> p t f", f=FA),
+            )
+
+        def ev_on_vector(n, s):
+            if n >= GROUPS - 2:
+                return s % 2 == 0
+            return n % 2 == 0 and s == 0
+
+        def evs(n):
+            for s in range(GROUP):
+                ev(n, s, ev_on_vector(n, s))
+
+        tr("w")
+        cp("w", 0, True)
+        cp("w", 1, False)
+        tr(0)
+        cp(0, 0, True)
+        cp(0, 1, False)
+        qz("w")
+        tr(1)
+        qz(0)
+        cp(1, 0, True)
+        cp(1, 1, False)
+        mx(0)
+        tr(2)
+        qz(1)
+        evs(0)
+        st(0)
+        cp(2, 0, True)
+        cp(2, 1, True)
+        for n in range(1, GROUPS):
+            if n + 2 < GROUPS:
+                tr(n + 2)
+                cp(n + 2, 0, True)
+            if n + 1 < GROUPS:
+                qz(n + 1)
+            mx(n)
+            if n + 2 < GROUPS:
+                cp(n + 2, 1, True)
+            evs(n)
+            st(n)

@@ -25,6 +25,7 @@ BYTES = N_TOK * K * 2 + FA * K * 2 + N_TOK * FA * 4
 
 PINNED = True
 LOADS = [(0, 4), (4, 8), (8, 12), (12, 16), (16, 24), (24, 32)]
+STORES = [(0, 4), (4, 8), (8, 12), (12, 16), (16, 20), (20, 24), (24, 26), (26, 28), (28, 30), (30, 31), (31, 32)]
 
 
 def tile_ssheaggregatorlayer_t_kernel(tc, xa, xb, y, wa, wb, grad_out, out):
@@ -115,18 +116,21 @@ def tile_ssheaggregatorlayer_t_kernel(tc, xa, xb, y, wa, wb, grad_out, out):
                 )
 
         def ev(n, s, on_vector):
-            if s == 0:
-                o_sb[n] = keep.tile([P, GROUP * FA], F32, name="o_sb%d" % n)
-            dst = o_sb[n][:, s * FA : (s + 1) * FA]
+            t = GROUP * n + s
+            for t0, t1 in STORES:
+                if t0 == t:
+                    o_sb[t0] = keep.tile([P, (t1 - t0) * FA], F32, name="o_sb%d" % t0)
+                if t0 <= t < t1:
+                    dst = o_sb[t0][:, (t - t0) * FA : (t - t0 + 1) * FA]
             if on_vector:
                 nc.vector.tensor_scalar_mul(out=dst, in0=accs[(n, s)][:], scalar1=0.25)
             else:
                 nc.scalar.activation(out=dst, in_=accs[(n, s)][:], func=COPY, scale=0.25)
 
-        def st(n):
+        def st(t0, t1):
             nc.sync.dma_start(
-                out=out_view[:, GROUP * n : GROUP * (n + 1), :],
-                in_=o_sb[n][:].rearrange("p (t f) -> p t f", f=FA),
+                out=out_view[:, t0:t1, :],
+                in_=o_sb[t0][:].rearrange("p (t f) -> p t f", f=FA),
             )
 
         def ev_on_vector(n, s):
@@ -137,6 +141,9 @@ def tile_ssheaggregatorlayer_t_kernel(tc, xa, xb, y, wa, wb, grad_out, out):
         def evs(n):
             for s in range(GROUP):
                 ev(n, s, ev_on_vector(n, s))
+                for t0, t1 in STORES:
+                    if t1 == GROUP * n + s + 1:
+                        st(t0, t1)
 
         tr("w")
         cp("w", 0, True)
@@ -153,7 +160,6 @@ def tile_ssheaggregatorlayer_t_kernel(tc, xa, xb, y, wa, wb, grad_out, out):
         tr(2)
         qz(1)
         evs(0)
-        st(0)
         cp(2, 0, True)
         cp(2, 1, True)
         for n in range(1, GROUPS):
@@ -166,4 +172,3 @@ def tile_ssheaggregatorlayer_t_kernel(tc, xa, xb, y, wa, wb, grad_out, out):
             if n + 2 < GROUPS:
                 cp(n + 2, 1, True)
             evs(n)
-            st(n)

@@ -24,8 +24,8 @@ FLOPS = 2 * N_TOK * K * FA
 BYTES = N_TOK * K * 2 + FA * K * 2 + N_TOK * FA * 4
 
 PINNED = True
-LOADS = [(0, 4), (4, 8), (8, 12), (12, 16), (16, 24), (24, 32)]
-STORES = [(0, 4), (4, 8), (8, 12), (12, 16), (16, 20), (20, 24), (24, 26), (26, 28), (28, 30), (30, 31), (31, 32)]
+LOADS = [(0, 4), (4, 8), (8, 16), (16, 24), (24, 32)]
+STORES = [(0, 4), (4, 8), (8, 12), (12, 16), (16, 20), (20, 24), (24, 32)]
 
 
 def tile_ssheaggregatorlayer_t_kernel(tc, xa, xb, y, wa, wb, grad_out, out):
@@ -41,10 +41,7 @@ def tile_ssheaggregatorlayer_t_kernel(tc, xa, xb, y, wa, wb, grad_out, out):
         out_view = out.rearrange("(p t) f -> p t f", t=TILES)
 
         w_sb = keep.tile([P, GROUP * K], BF16, name="w_sb")
-        nc.sync.dma_start(
-            out=w_sb[:].rearrange("p (j o) -> p j o", o=K),
-            in_=wa.rearrange("(j p) o -> p j o", p=P),
-        )
+        nc.sync.dma_start(out=w_sb[:], in_=wa.rearrange("(p j) o -> p (j o)", j=GROUP))
         src_of_tile = {}
         for c, (t0, t1) in enumerate(LOADS):
             g_sb = keep.tile([P, (t1 - t0) * K], BF16, name="g_sb%d" % c)
@@ -86,9 +83,13 @@ def tile_ssheaggregatorlayer_t_kernel(tc, xa, xb, y, wa, wb, grad_out, out):
                         nc.tensor.transpose(xt[:, s, u, :], words[:, col : col + P], ident[:])
 
         def cp(n, h, on_vector):
-            dst = grouped[n][:].bitcast(F32)[:, h * K : (h + 1) * K]
-            dst = dst.rearrange("p (s n u) -> p s n u", s=2, u=2)
-            src = banks[(n, h)][:].rearrange("p s u n -> p s n u")
+            if n == "w":
+                dst = grouped[n][:].bitcast(F32).rearrange("k (p h s u) -> k h p s u", h=2, s=2, u=2)[:, h]
+                src = banks[(n, h)][:].rearrange("k s u p -> k p s u")
+            else:
+                dst = grouped[n][:].bitcast(F32)[:, h * K : (h + 1) * K]
+                dst = dst.rearrange("p (s n u) -> p s n u", s=2, u=2)
+                src = banks[(n, h)][:].rearrange("p s u n -> p s n u")
             if on_vector:
                 nc.vector.tensor_copy(out=dst, in_=src)
             else:
@@ -147,7 +148,7 @@ def tile_ssheaggregatorlayer_t_kernel(tc, xa, xb, y, wa, wb, grad_out, out):
 
         tr("w")
         cp("w", 0, True)
-        cp("w", 1, False)
+        cp("w", 1, True)
         tr(0)
         cp(0, 0, True)
         cp(0, 1, False)

@@ -25,7 +25,7 @@ BYTES = N_TOK * K * 2 + FA * K * 2 + N_TOK * FA * 4
 
 PINNED = True
 LOADS = [(0, 4), (4, 8), (8, 16), (16, 24), (24, 32)]
-STORES = [(0, 4), (4, 8), (8, 12), (12, 16), (16, 20), (20, 24), (24, 32)]
+STORES = [(0, 4), (4, 8), (8, 12), (12, 16), (16, 20), (20, 24), (24, 28), (28, 32)]
 
 
 def tile_ssheaggregatorlayer_t_kernel(tc, xa, xb, y, wa, wb, grad_out, out):
@@ -134,42 +134,37 @@ def tile_ssheaggregatorlayer_t_kernel(tc, xa, xb, y, wa, wb, grad_out, out):
                 in_=o_sb[t0][:].rearrange("p (t f) -> p t f", f=FA),
             )
 
-        def ev_on_vector(n, s):
-            if n >= GROUPS - 2:
-                return s % 2 == 0
-            return n % 2 == 0 and s == 0
-
-        def evs(n):
-            for s in range(GROUP):
-                ev(n, s, ev_on_vector(n, s))
-                for t0, t1 in STORES:
-                    if t1 == GROUP * n + s + 1:
-                        st(t0, t1)
+        def stores_ending_in(n):
+            for t0, t1 in STORES:
+                if GROUP * n < t1 <= GROUP * (n + 1):
+                    st(t0, t1)
 
         tr("w")
         cp("w", 0, True)
         cp("w", 1, True)
-        tr(0)
-        cp(0, 0, True)
-        cp(0, 1, False)
         qz("w")
-        tr(1)
+        tr(0)
+        cp(0, 0, False)
+        cp(0, 1, False)
         qz(0)
-        cp(1, 0, True)
+        tr(1)
+        cp(1, 0, False)
         cp(1, 1, False)
-        mx(0)
-        tr(2)
-        qz(1)
-        evs(0)
-        cp(2, 0, True)
-        cp(2, 1, True)
-        for n in range(1, GROUPS):
-            if n + 2 < GROUPS:
-                tr(n + 2)
-                cp(n + 2, 0, True)
+        for n in range(GROUPS):
             if n + 1 < GROUPS:
                 qz(n + 1)
             mx(n)
             if n + 2 < GROUPS:
+                tr(n + 2)
+                ev(n, 0, False)
+                ev(n, 1, False)
+                ev(n, 2, True)
+                ev(n, 3, n % 2 == 0)
+                cp(n + 2, 0, False)
                 cp(n + 2, 1, True)
-            evs(n)
+            else:
+                ev(n, 0, False)
+                ev(n, 1, True)
+                ev(n, 2, False)
+                ev(n, 3, True)
+            stores_ending_in(n)

@@ -52,6 +52,8 @@ def tile_ssheaggregatorlayer_t_kernel(tc, xa, xb, y, wa, wb, grad_out, out):
             for t in range(t0, t1):
                 src_of_tile[t] = (g_sb[:].bitcast(F32), t - t0)
 
+        zeros = keep.tile([P, FA], BF16, name="zeros")
+        nc.vector.memset(zeros[:], 0.0)
         ident = keep.tile([P, P], F32, name="ident")
         make_identity(nc, ident[:])
         warm = keep.tile([P, 8], F32, name="warm")
@@ -134,20 +136,29 @@ def tile_ssheaggregatorlayer_t_kernel(tc, xa, xb, y, wa, wb, grad_out, out):
                 in_=o_sb[t0][:].rearrange("p (t f) -> p t f", f=FA),
             )
 
+        def dummies(count):
+            for i in range(count):
+                acc = acc_pool.tile([P, FA], F32, name="acc")
+                nc.tensor.matmul(out=acc[:], lhsT=zeros[:, 0:P], rhs=zeros[:], start=True, stop=True)
+
         def stores_ending_in(n):
             for t0, t1 in STORES:
                 if GROUP * n < t1 <= GROUP * (n + 1):
                     st(t0, t1)
 
+        dummies(6)
         tr("w")
+        dummies(1)
         cp("w", 0, True)
         cp("w", 1, True)
         qz("w")
         tr(0)
+        dummies(1)
         cp(0, 0, False)
         cp(0, 1, False)
         qz(0)
         tr(1)
+        dummies(2)
         cp(1, 0, False)
         cp(1, 1, False)
         for n in range(GROUPS):

@@ -162,20 +162,18 @@ def tile_ssheaggregatorlayer_t_kernel(tc, xa, xb, y, wa, wb, grad_out, out):
         cp(1, 0, False)
         cp(1, 1, False)
         for n in range(GROUPS):
-            if n + 1 < GROUPS:
-                qz(n + 1)
             mx(n)
             if n + 2 < GROUPS:
                 tr(n + 2)
-                ev(n, 0, False)
-                ev(n, 1, False)
-                ev(n, 2, True)
+            ev(n, 0, False)
+            ev(n, 1, True)
+            if n + 1 < GROUPS:
+                qz(n + 1)
+            ev(n, 2, False)
+            if n + 2 < GROUPS:
                 ev(n, 3, n % 2 == 0)
                 cp(n + 2, 0, False)
                 cp(n + 2, 1, True)
             else:
-                ev(n, 0, False)
-                ev(n, 1, True)
-                ev(n, 2, False)
                 ev(n, 3, True)
             stores_ending_in(n)

@@ -24,7 +24,7 @@ FLOPS = 2 * N_TOK * K * FA
 BYTES = N_TOK * K * 2 + FA * K * 2 + N_TOK * FA * 4
 
 PINNED = True
-LOADS = [(0, 4), (4, 8), (8, 16), (16, 24), (24, 32)]
+LOADS = [(0, 4), (4, 8), (8, 16), (16, 32)]
 STORES = [(0, 4), (4, 8), (8, 12), (12, 16), (16, 20), (20, 24), (24, 28), (28, 32)]
 
 
@@ -118,17 +118,17 @@ def tile_ssheaggregatorlayer_t_kernel(tc, xa, xb, y, wa, wb, grad_out, out):
                     stop=True,
                 )
 
-        def ev(n, s, on_vector):
+        def ev(n, s, on_vector, c0=0, c1=FA):
             t = GROUP * n + s
             for t0, t1 in STORES:
-                if t0 == t:
+                if t0 == t and c0 == 0:
                     o_sb[t0] = keep.tile([P, (t1 - t0) * FA], F32, name="o_sb%d" % t0)
                 if t0 <= t < t1:
-                    dst = o_sb[t0][:, (t - t0) * FA : (t - t0 + 1) * FA]
+                    dst = o_sb[t0][:, (t - t0) * FA + c0 : (t - t0) * FA + c1]
             if on_vector:
-                nc.vector.tensor_scalar_mul(out=dst, in0=accs[(n, s)][:], scalar1=0.25)
+                nc.vector.tensor_scalar_mul(out=dst, in0=accs[(n, s)][:, c0:c1], scalar1=0.25)
             else:
-                nc.scalar.activation(out=dst, in_=accs[(n, s)][:], func=COPY, scale=0.25)
+                nc.scalar.activation(out=dst, in_=accs[(n, s)][:, c0:c1], func=COPY, scale=0.25)
 
         def st(t0, t1):
             nc.sync.dma_start(
@@ -171,7 +171,8 @@ def tile_ssheaggregatorlayer_t_kernel(tc, xa, xb, y, wa, wb, grad_out, out):
                 qz(n + 1)
             ev(n, 2, False)
             if n + 2 < GROUPS:
-                ev(n, 3, n % 2 == 0)
+                ev(n, 3, False, 0, FA // 2)
+                ev(n, 3, True, FA // 2, FA)
                 cp(n + 2, 0, False)
                 cp(n + 2, 1, True)
             else:

from contextlib import ExitStack

import concourse.mybir as mybir
from concourse.masks import make_identity

F32 = mybir.dt.float32
BF16 = mybir.dt.bfloat16
U32 = mybir.dt.uint32
U8 = mybir.dt.uint8
E4M3X4 = mybir.dt.float8_e4m3fn_x4
E5M2X4 = mybir.dt.float8_e5m2_x4
COPY = mybir.ActivationFunctionType.Copy

P = 128
N_TOK = 4096
K = 512
FA = 512
TILES = N_TOK // P
GROUP = 4
GROUPS = TILES // GROUP
WORDS = K // 2

FLOPS = 2 * N_TOK * K * FA
BYTES = N_TOK * K * 2 + FA * K * 2 + N_TOK * FA * 4

PINNED = True
LOADS = [(0, 4), (4, 8), (8, 16), (16, 32)]
STORES = [(0, 4), (4, 8), (8, 12), (12, 16), (16, 20), (20, 24), (24, 28), (28, 32)]


def tile_ssheaggregatorlayer_t_kernel(tc, xa, xb, y, wa, wb, grad_out, out):
    nc = tc.nc
    with ExitStack() as ctx:
        keep = ctx.enter_context(tc.tile_pool(name="keep", bufs=1))
        xt_pool = ctx.enter_context(tc.psum_pool(name="xtp", bufs=4))
        acc_pool = ctx.enter_context(tc.psum_pool(name="accp", bufs=4))
        if PINNED:
            ctx.enter_context(tc.manual_schedule())

        g_view = grad_out.rearrange("(p t) o -> p t o", t=TILES)
        out_view = out.rearrange("(p t) f -> p t f", t=TILES)

        w_sb = keep.tile([P, GROUP * K], BF16, name="w_sb")
        nc.sync.dma_start(out=w_sb[:], in_=wa.rearrange("(p j) o -> p (j o)", j=GROUP))
        src_of_tile = {}
        for c, (t0, t1) in enumerate(LOADS):
            g_sb = keep.tile([P, (t1 - t0) * K], BF16, name="g_sb%d" % c)
            nc.sync.dma_start(
                out=g_sb[:].rearrange("p (t o) -> p t o", o=K),
                in_=g_view[:, t0:t1, :],
            )
            for t in range(t0, t1):
                src_of_tile[t] = (g_sb[:].bitcast(F32), t - t0)

        zeros = keep.tile([P, FA], BF16, name="zeros")
        nc.vector.memset(zeros[:], 0.0)
        ident = keep.tile([P, P], F32, name="ident")
        make_identity(nc, ident[:])
        warm = keep.tile([P, 8], F32, name="warm")
        nc.vector.memset(warm[:], 0.0)
        nc.scalar.activation(out=warm[:], in_=warm[:], func=COPY, scale=0.25)

        w_words = w_sb[:].bitcast(F32)
        banks = {}
        grouped = {}
        codes = {}
        scales = {}
        accs = {}
        o_sb = {}

        def source(n, s):
            if n == "w":
                return w_words, s
            return src_of_tile[GROUP * n + s]

        def tr(n):
            grouped[n] = keep.tile([P, GROUP * K], BF16, name="grouped_%s" % n, align_bytes=64)
            for h in range(2):
                xt = xt_pool.tile([P, 2, 2, P], F32, name="xt")
                banks[(n, h)] = xt
                for s in range(2):
                    words, local = source(n, 2 * h + s)
                    for u in range(2):
                        col = local * WORDS + u * P
                        nc.tensor.transpose(xt[:, s, u, :], words[:, col : col + P], ident[:])

        def cp(n, h, on_vector):
            if n == "w":
                dst = grouped[n][:].bitcast(F32).rearrange("k (p h s u) -> k h p s u", h=2, s=2, u=2)[:, h]
                src = banks[(n, h)][:].rearrange("k s u p -> k p s u")
            else:
                dst = grouped[n][:].bitcast(F32)[:, h * K : (h + 1) * K]
                dst = dst.rearrange("p (s n u) -> p s n u", s=2, u=2)
                src = banks[(n, h)][:].rearrange("p s u n -> p s n u")
            if on_vector:
                nc.vector.tensor_copy(out=dst, in_=src)
            else:
                nc.scalar.copy(out=dst, in_=src)

        def qz(n):
            codes[n] = keep.tile([P, GROUP * P], U32, name="codes_%s" % n, align_bytes=64)
            scales[n] = keep.tile([P, GROUP * P], U8, name="scales_%s" % n, align_bytes=64)
            fmt = E4M3X4 if n == "w" else E5M2X4
            nc.vector.quantize_mx(out=codes[n][:].bitcast(fmt), scales=scales[n][:], in_=grouped[n][:])

        def mx(n):
            for s in range(GROUP):
                acc = acc_pool.tile([P, FA], F32, name="acc")
                accs[(n, s)] = acc
                cols = slice(s * P, (s + 1) * P)
                nc.tensor.matmul_mx(
                    out=acc[:],
                    lhsT=codes[n][:, cols].bitcast(E5M2X4),
                    lhsT_scale=scales[n][:, cols],
                    rhs=codes["w"][:].bitcast(E4M3X4),
                    rhs_scale=scales["w"][:],
                    start=True,
                    stop=True,
                )

        def ev(n, s, on_vector, c0=0, c1=FA):
            t = GROUP * n + s
            for t0, t1 in STORES:
                if t0 == t and c0 == 0:
                    o_sb[t0] = keep.tile([P, (t1 - t0) * FA], F32, name="o_sb%d" % t0)
                if t0 <= t < t1:
                    dst = o_sb[t0][:, (t - t0) * FA + c0 : (t - t0) * FA + c1]
            if on_vector:
                nc.vector.tensor_scalar_mul(out=dst, in0=accs[(n, s)][:, c0:c1], scalar1=0.25)
            else:
                nc.scalar.activation(out=dst, in_=accs[(n, s)][:, c0:c1], func=COPY, scale=0.25)

        def st(t0, t1):
            nc.sync.dma_start(
                out=out_view[:, t0:t1, :],
                in_=o_sb[t0][:].rearrange("p (t f) -> p t f", f=FA),
            )

        def dummies(count):
            for i in range(count):
                acc = acc_pool.tile([P, FA], F32, name="acc")
                nc.tensor.matmul(out=acc[:], lhsT=zeros[:, 0:P], rhs=zeros[:], start=True, stop=True)

        def stores_ending_in(n):
            for t0, t1 in STORES:
                if GROUP * n < t1 <= GROUP * (n + 1):
                    st(t0, t1)

        dummies(6)
        tr("w")
        dummies(1)
        cp("w", 0, True)
        cp("w", 1, True)
        qz("w")
        tr(0)
        dummies(1)
        cp(0, 0, False)
        cp(0, 1, False)
        qz(0)
        tr(1)
        dummies(2)
        cp(1, 0, False)
        cp(1, 1, False)
        for n in range(GROUPS):
            mx(n)
            if n + 2 < GROUPS:
                tr(n + 2)
            ev(n, 0, False)
            ev(n, 1, True)
            if n + 1 < GROUPS:
                qz(n + 1)
            ev(n, 2, False)
            if n + 2 < GROUPS:
                ev(n, 3, False, 0, FA // 2)
                ev(n, 3, True, FA // 2, FA)
                cp(n + 2, 0, False)
                cp(n + 2, 1, True)
            else:
                ev(n, 3, True)
            stores_ending_in(n)
